import numpy as np
import ml_dtypes


def mxq(x, axis, fmt="e4m3"):
    dtype, down = {"e4m3": (ml_dtypes.float8_e4m3fn, 7), "e5m2": (ml_dtypes.float8_e5m2, 14)}[fmt]
    v = np.moveaxis(np.asarray(x, np.float32).astype(ml_dtypes.bfloat16).astype(np.float64), axis, -1)
    blocks = v.reshape(v.shape[:-1] + (-1, 32))
    amax = np.abs(blocks).max(-1, keepdims=True)
    byte = np.maximum(np.where(amax > 0, np.frexp(amax)[1] - 1 + 127, 0) - down, 1)
    scale = np.exp2(byte - 127.0)
    codes = (blocks / scale).astype(np.float32).astype(dtype).astype(np.float64)
    return np.moveaxis((codes * scale).reshape(v.shape), -1, axis)


WIDE = False


def mx_kscale(k):
    if not WIDE:
        return np.ones(k)
    levels = np.array([10, -10, 5, -5, 0])
    a = np.random.permutation(np.resize(levels, k // 512 * 4)).reshape(k // 512, 4)
    idx = np.arange(k)
    return np.exp2(a[idx // 512, idx % 128 // 32])


BF16 = ml_dtypes.bfloat16


def bf(x):
    return np.asarray(x, np.float32).astype(BF16)


def f64(x):
    return np.asarray(x).astype(np.float64)


B, IN, L = 4096, 1024, 256


def sigmoid(v):
    return 1.0 / (1.0 + np.exp(-v))


def setup_inputs():
    s = mx_kscale(IN)
    return {"input": bf(np.random.standard_normal((B, IN)) * s),
            "h0": bf(np.random.standard_normal((B, L))),
            "gh0": bf(np.random.standard_normal((B, 3 * L)) * 0.75),
            "W_ih0": bf(np.random.standard_normal((3 * L, IN)) * 0.7 / np.sqrt(IN) / s),
            "b_ih0": bf(np.random.standard_normal(3 * L) * 0.3)}


def reference(input, h0, gh0, W_ih0, b_ih0):
    h, gh = f64(h0), f64(gh0)
    gi = (mxq(f64(input), 1, "e4m3") @ mxq(f64(W_ih0), 1, "e4m3").T) + f64(b_ih0)
    i_r, i_z, i_n = gi[:, :L], gi[:, L:2 * L], gi[:, 2 * L:]
    h_r, h_z, h_n = gh[:, :L], gh[:, L:2 * L], gh[:, 2 * L:]
    r = sigmoid(i_r + h_r)
    z = sigmoid(i_z + h_z)
    n = np.tanh(i_n + r * h_n)
    return (1.0 - z) * n + z * h

@@ -1,0 +1,224 @@
+from contextlib import ExitStack
+
+import concourse.bass as bass
+import concourse.mybir as mybir
+import concourse.tile as tile
+from concourse.masks import make_identity
+
+F32 = mybir.dt.float32
+BF16 = mybir.dt.bfloat16
+U32 = mybir.dt.uint32
+U8 = mybir.dt.uint8
+FP8X4 = mybir.dt.float8_e4m3fn_x4
+ACT = mybir.ActivationFunctionType
+ALU = mybir.AluOpType
+
+P = 128
+B = 4096
+IN = 1024
+L = 256
+G3 = 3 * L
+NT = B // P
+GRP = 4
+NG = NT // GRP
+WT = G3 // P
+
+FLOPS = 2 * B * IN * G3
+
+V_TAIL_GROUPS = (7,)
+
+
+def tile_grucellstack_pa_t_kernel(tc, x, h0, gh0, w_ih0, b_ih0, out):
+    nc = tc.nc
+    x_v = x.rearrange("(p t) k -> p (t k)", t=NT)
+    g_v = gh0.rearrange("(p t) c -> p t c", t=NT)
+    h_v = h0.rearrange("(p t) c -> p t c", t=NT)
+    o_v = out.rearrange("(p t) c -> p t c", t=NT)
+    w_v = w_ih0.rearrange("(t p) k -> p t k", p=P)
+
+    with ExitStack() as ctx:
+        const = ctx.enter_context(tc.tile_pool(name="const", bufs=1))
+        xin = ctx.enter_context(tc.tile_pool(name="xin", bufs=NG))
+        gin = ctx.enter_context(tc.tile_pool(name="gin", bufs=NG))
+        hin = ctx.enter_context(tc.tile_pool(name="hin", bufs=NG))
+        grp = ctx.enter_context(tc.tile_pool(name="grp", bufs=4))
+        cod = ctx.enter_context(tc.tile_pool(name="cod", bufs=8))
+        rzp = ctx.enter_context(tc.tile_pool(name="rzp", bufs=4))
+        upl = ctx.enter_context(tc.tile_pool(name="upl", bufs=3))
+        opl = ctx.enter_context(tc.tile_pool(name="opl", bufs=4))
+        pbias = ctx.enter_context(tc.psum_pool(name="pbias", bufs=1))
+        pxt = ctx.enter_context(tc.psum_pool(name="pxt", bufs=2))
+        pzz = ctx.enter_context(tc.psum_pool(name="pzz", bufs=2))
+        pnn = ctx.enter_context(tc.psum_pool(name="pnn", bufs=2))
+
+        bz = const.tile([P, G3], BF16)
+        nc.vector.memset(bz[:], 0.0)
+        ones = const.tile([P, P], BF16)
+        nc.vector.memset(ones[:], 1.0)
+        ident = const.tile([P, P], F32)
+        make_identity(nc, ident[:])
+
+        nc.sync.dma_start(out=bz[0:1, :], in_=b_ih0.rearrange("(o c) -> o c", o=1))
+        x_sb = []
+        g_sb = []
+        h_sb = []
+        w_sb = const.tile([P, WT, IN], BF16)
+
+        def load_x(c):
+            xt_in = xin.tile([P, GRP * IN], BF16)
+            nc.sync.dma_start(out=xt_in[:], in_=x_v[:, c * GRP * IN:(c + 1) * GRP * IN])
+            x_sb.append(xt_in)
+
+        def load_g(c):
+            gt_in = gin.tile([P, GRP, G3], BF16)
+            nc.sync.dma_start(out=gt_in[:], in_=g_v[:, c * GRP:(c + 1) * GRP, :])
+            g_sb.append(gt_in)
+
+        def load_h(c):
+            ht_in = hin.tile([P, GRP, L], BF16)
+            nc.sync.dma_start(out=ht_in[:], in_=h_v[:, c * GRP:(c + 1) * GRP, :])
+            h_sb.append(ht_in)
+
+        load_g(0)
+        load_x(0)
+        for i in range(3):
+            nc.sync.dma_start(out=w_sb[:, 2 * i:2 * i + 2, :], in_=w_v[:, 2 * i:2 * i + 2, :])
+        load_g(1)
+        load_x(1)
+        load_h(0)
+        for c in range(2, NG):
+            load_g(c)
+            load_x(c)
+            load_h(c - 1)
+        load_h(NG - 1)
+
+        bp_rz = pbias.tile([P, 2 * L], F32)
+        bp_n = pbias.tile([P, L], F32)
+        nc.tensor.matmul(out=bp_rz[:], lhsT=ones[:], rhs=bz[:, 0:2 * L], start=True, stop=True)
+        nc.tensor.matmul(out=bp_n[:], lhsT=ones[:], rhs=bz[:, 2 * L:G3], start=True, stop=True)
+
+        wcodes = const.tile([P, 2 * G3], U32, align_bytes=64)
+        wscl = const.tile([P, 2 * G3], U8, align_bytes=64)
+
+        def turn(words, col0, copy_engine):
+            xt = pxt.tile([P, 4, P], F32)
+            for q in range(4):
+                nc.tensor.transpose(xt[:, q, :], words[:, col0 + q * P:col0 + (q + 1) * P], ident[:])
+            grouped = grp.tile([P, 2 * P * 4], BF16, align_bytes=64)
+            dst = grouped[:].bitcast(F32).rearrange("p (g r u) -> p g r u", g=2, u=2)
+            src = xt[:].rearrange("p (g u) r -> p g r u", u=2)
+            if copy_engine == "v":
+                nc.vector.tensor_copy(out=dst, in_=src)
+            else:
+                nc.scalar.copy(out=dst, in_=src)
+            return grouped
+
+        def prep_w(lt):
+            ww = w_sb[:, lt, :].bitcast(F32)
+            grouped = turn(ww, 0, "v" if lt % 2 else "s")
+            for g in range(2):
+                c0 = g * G3 + lt * P
+                nc.vector.quantize_mx(
+                    out=wcodes[:, c0:c0 + P].bitcast(FP8X4),
+                    scales=wscl[:, c0:c0 + P],
+                    in_=grouped[:, g * 4 * P:(g + 1) * 4 * P],
+                )
+
+        xcodes = {}
+
+        def prep_x(c):
+            xw = x_sb[c][:].bitcast(F32)
+            for j in range(GRP):
+                grouped = turn(xw, j * (IN // 2), "s")
+                codes = cod.tile([P, 2 * P], U32, align_bytes=64)
+                scl = cod.tile([P, 2 * P], U8, align_bytes=64)
+                nc.vector.quantize_mx(out=codes[:].bitcast(FP8X4), scales=scl[:], in_=grouped[:])
+                xcodes[(c, j)] = (codes, scl)
+
+        rz_t = {}
+        u_t = {}
+        pn_t = {}
+
+        def e1(c):
+            rz = rzp.tile([P, GRP, 2 * L], F32)
+            nc.vector.tensor_tensor(
+                out=rz[:],
+                in0=g_sb[c][:, :, 0:2 * L],
+                in1=bp_rz[:].unsqueeze(1).to_broadcast([P, GRP, 2 * L]),
+                op=ALU.add,
+            )
+            rz_t[c] = rz
+
+        def main(c):
+            rz = rz_t[c]
+            for j in range(GRP):
+                codes, scl = xcodes[(c, j)]
+                prz = pzz.tile([P, 2 * L], F32)
+                if j % 2 == 0:
+                    pn = pnn.tile([P, 2, L], F32)
+                    pn_t[(c, j // 2)] = pn
+                pn = pn_t[(c, j // 2)]
+                for g in range(2):
+                    lhs = codes[:, g * P:(g + 1) * P].bitcast(FP8X4)
+                    lsc = scl[:, g * P:(g + 1) * P]
+                    nc.tensor.matmul_mx(
+                        out=prz[:], lhsT=lhs, lhsT_scale=lsc,
+                        rhs=wcodes[:, g * G3:g * G3 + 2 * L].bitcast(FP8X4),
+                        rhs_scale=wscl[:, g * G3:g * G3 + 2 * L],
+                        start=(g == 0), stop=(g == 1),
+                    )
+                    nc.tensor.matmul_mx(
+                        out=pn[:, j % 2, :], lhsT=lhs, lhsT_scale=lsc,
+                        rhs=wcodes[:, g * G3 + 2 * L:(g + 1) * G3].bitcast(FP8X4),
+                        rhs_scale=wscl[:, g * G3 + 2 * L:(g + 1) * G3],
+                        start=(g == 0), stop=(g == 1),
+                    )
+                nc.vector.tensor_tensor(out=rz[:, j, :], in0=prz[:], in1=rz[:, j, :], op=ALU.add)
+                nc.scalar.activation(out=rz[:, j, :], in_=rz[:, j, :], func=ACT.Sigmoid)
+
+        def mid(c):
+            rz = rz_t[c]
+            u = upl.tile([P, GRP, L], F32)
+            u_t[c] = u
+            for h in range(GRP // 2):
+                js = slice(2 * h, 2 * h + 2)
+                nc.vector.tensor_tensor(out=u[:, js, :], in0=rz[:, js, 0:L], in1=g_sb[c][:, js, 2 * L:G3], op=ALU.mult)
+                nc.vector.tensor_tensor(out=u[:, js, :], in0=pn_t[(c, h)][:], in1=u[:, js, :], op=ALU.add)
+                nc.vector.tensor_tensor(
+                    out=u[:, js, :],
+                    in0=bp_n[:].unsqueeze(1).to_broadcast([P, 2, L]),
+                    in1=u[:, js, :],
+                    op=ALU.add,
+                )
+                nc.scalar.activation(out=u[:, js, :], in_=u[:, js, :], func=ACT.Tanh)
+
+        def tail(c):
+            rz = rz_t[c]
+            u = u_t[c]
+            o = opl.tile([P, GRP, L], F32)
+            if c in V_TAIL_GROUPS:
+                for h in range(GRP // 2):
+                    js = slice(2 * h, 2 * h + 2)
+                    nc.vector.tensor_tensor(out=o[:, js, :], in0=h_sb[c][:, js, :], in1=u[:, js, :], op=ALU.subtract)
+                    nc.vector.tensor_tensor(out=o[:, js, :], in0=o[:, js, :], in1=rz[:, js, L:2 * L], op=ALU.mult)
+                    nc.vector.tensor_tensor(out=o[:, js, :], in0=o[:, js, :], in1=u[:, js, :], op=ALU.add)
+                    nc.sync.dma_start(out=o_v[:, c * GRP + 2 * h:c * GRP + 2 * h + 2, :], in_=o[:, js, :])
+            else:
+                nc.gpsimd.tensor_tensor(out=o[:], in0=h_sb[c][:], in1=u[:], op=ALU.subtract)
+                nc.gpsimd.tensor_tensor(out=o[:], in0=o[:], in1=rz[:, :, L:2 * L], op=ALU.mult)
+                nc.gpsimd.tensor_tensor(out=o[:], in0=o[:], in1=u[:], op=ALU.add)
+                nc.sync.dma_start(out=o_v[:, c * GRP:(c + 1) * GRP, :], in_=o[:])
+
+        e1(0)
+        prep_x(0)
+        for lt in range(WT):
+            prep_w(lt)
+        e1(1)
+        prep_x(1)
+        for c in range(NG):
+            main(c)
+            if c + 2 < NG:
+                e1(c + 2)
+                prep_x(c + 2)
+            mid(c)
+            tail(c)

@@ -1,8 +1,6 @@
 from contextlib import ExitStack
 
-import concourse.bass as bass
 import concourse.mybir as mybir
-import concourse.tile as tile
 from concourse.masks import make_identity
 
 F32 = mybir.dt.float32
@@ -22,10 +20,10 @@ NT = B // P
 GRP = 4
 NG = NT // GRP
 WT = G3 // P
+PIN = True
+V_COPY_UNTIL = 4
 
 FLOPS = 2 * B * IN * G3
-
-V_TAIL_GROUPS = (7,)
 
 
 def tile_grucellstack_pa_t_kernel(tc, x, h0, gh0, w_ih0, b_ih0, out):
@@ -35,190 +33,245 @@ def tile_grucellstack_pa_t_kernel(tc, x, h0, gh0, w_ih0, b_ih0, out):
     h_v = h0.rearrange("(p t) c -> p t c", t=NT)
     o_v = out.rearrange("(p t) c -> p t c", t=NT)
     w_v = w_ih0.rearrange("(t p) k -> p t k", p=P)
+    n = GRP * P
 
     with ExitStack() as ctx:
+        if PIN:
+            ctx.enter_context(tc.manual_schedule())
         const = ctx.enter_context(tc.tile_pool(name="const", bufs=1))
-        xin = ctx.enter_context(tc.tile_pool(name="xin", bufs=NG))
+        xin = ctx.enter_context(tc.tile_pool(name="xin", bufs=4))
         gin = ctx.enter_context(tc.tile_pool(name="gin", bufs=NG))
         hin = ctx.enter_context(tc.tile_pool(name="hin", bufs=NG))
-        grp = ctx.enter_context(tc.tile_pool(name="grp", bufs=4))
-        cod = ctx.enter_context(tc.tile_pool(name="cod", bufs=8))
-        rzp = ctx.enter_context(tc.tile_pool(name="rzp", bufs=4))
-        upl = ctx.enter_context(tc.tile_pool(name="upl", bufs=3))
-        opl = ctx.enter_context(tc.tile_pool(name="opl", bufs=4))
-        pbias = ctx.enter_context(tc.psum_pool(name="pbias", bufs=1))
+        grp = ctx.enter_context(tc.tile_pool(name="grp", bufs=2))
+        cod = ctx.enter_context(tc.tile_pool(name="cod", bufs=3))
+        pbp = ctx.enter_context(tc.tile_pool(name="pbp", bufs=2))
+        rzp = ctx.enter_context(tc.tile_pool(name="rzp", bufs=3))
+        vpl = ctx.enter_context(tc.tile_pool(name="vpl", bufs=4))
+        upl = ctx.enter_context(tc.tile_pool(name="upl", bufs=2))
+        opl = ctx.enter_context(tc.tile_pool(name="opl", bufs=3))
         pxt = ctx.enter_context(tc.psum_pool(name="pxt", bufs=2))
-        pzz = ctx.enter_context(tc.psum_pool(name="pzz", bufs=2))
+        ppt = ctx.enter_context(tc.psum_pool(name="ppt", bufs=2))
+        pac = ctx.enter_context(tc.psum_pool(name="pac", bufs=2))
         pnn = ctx.enter_context(tc.psum_pool(name="pnn", bufs=2))
 
-        bz = const.tile([P, G3], BF16)
+        brow = const.tile([P, P], BF16)
+        nc.vector.memset(brow[:], 0.0)
+        bz = const.tile([P, L], BF16)
         nc.vector.memset(bz[:], 0.0)
         ones = const.tile([P, P], BF16)
         nc.vector.memset(ones[:], 1.0)
         ident = const.tile([P, P], F32)
         make_identity(nc, ident[:])
+        identb = const.tile([P, P], BF16)
+        make_identity(nc, identb[:])
 
-        nc.sync.dma_start(out=bz[0:1, :], in_=b_ih0.rearrange("(o c) -> o c", o=1))
-        x_sb = []
-        g_sb = []
-        h_sb = []
+        x_sb = {}
+        g_sb = {}
+        h_sb = {}
         w_sb = const.tile([P, WT, IN], BF16)
 
         def load_x(c):
             xt_in = xin.tile([P, GRP * IN], BF16)
             nc.sync.dma_start(out=xt_in[:], in_=x_v[:, c * GRP * IN:(c + 1) * GRP * IN])
-            x_sb.append(xt_in)
+            x_sb[c] = xt_in
 
-        def load_g(c):
+        def load_gh(c):
             gt_in = gin.tile([P, GRP, G3], BF16)
             nc.sync.dma_start(out=gt_in[:], in_=g_v[:, c * GRP:(c + 1) * GRP, :])
-            g_sb.append(gt_in)
-
-        def load_h(c):
+            g_sb[c] = gt_in
             ht_in = hin.tile([P, GRP, L], BF16)
             nc.sync.dma_start(out=ht_in[:], in_=h_v[:, c * GRP:(c + 1) * GRP, :])
-            h_sb.append(ht_in)
+            h_sb[c] = ht_in
 
-        load_g(0)
+        nc.sync.dma_start(out=brow[0:WT, :], in_=b_ih0.rearrange("(r c) -> r c", c=P))
+        nc.sync.dma_start(out=bz[0:1, :], in_=b_ih0.rearrange("(o c) -> o c", o=1)[:, 2 * L:G3])
         load_x(0)
         for i in range(3):
             nc.sync.dma_start(out=w_sb[:, 2 * i:2 * i + 2, :], in_=w_v[:, 2 * i:2 * i + 2, :])
-        load_g(1)
         load_x(1)
-        load_h(0)
-        for c in range(2, NG):
-            load_g(c)
-            load_x(c)
-            load_h(c - 1)
-        load_h(NG - 1)
+        load_gh(0)
+        load_x(2)
+        load_gh(1)
+        load_x(3)
 
-        bp_rz = pbias.tile([P, 2 * L], F32)
-        bp_n = pbias.tile([P, L], F32)
-        nc.tensor.matmul(out=bp_rz[:], lhsT=ones[:], rhs=bz[:, 0:2 * L], start=True, stop=True)
-        nc.tensor.matmul(out=bp_n[:], lhsT=ones[:], rhs=bz[:, 2 * L:G3], start=True, stop=True)
+        bt_ps = pxt.tile([P, P], BF16, tag="xt")
+        nc.tensor.transpose(bt_ps[:], brow[:], identb[:])
+        bias_col = const.tile([P, 8], F32)
+        nc.vector.tensor_copy(out=bias_col[:, 0:WT], in_=bt_ps[:, 0:WT])
+        bn_ps = pxt.tile([P, L], F32, tag="xt")
+        nc.tensor.matmul(out=bn_ps[:], lhsT=ones[:], rhs=bz[:], start=True, stop=True)
+        bn_sb = const.tile([P, L], F32)
+        nc.vector.tensor_copy(out=bn_sb[:], in_=bn_ps[:])
 
         wcodes = const.tile([P, 2 * G3], U32, align_bytes=64)
         wscl = const.tile([P, 2 * G3], U8, align_bytes=64)
 
-        def turn(words, col0, copy_engine):
+        def turn(words, col0, dst, on_vector):
             xt = pxt.tile([P, 4, P], F32)
             for q in range(4):
                 nc.tensor.transpose(xt[:, q, :], words[:, col0 + q * P:col0 + (q + 1) * P], ident[:])
-            grouped = grp.tile([P, 2 * P * 4], BF16, align_bytes=64)
-            dst = grouped[:].bitcast(F32).rearrange("p (g r u) -> p g r u", g=2, u=2)
             src = xt[:].rearrange("p (g u) r -> p g r u", u=2)
-            if copy_engine == "v":
+            if on_vector:
                 nc.vector.tensor_copy(out=dst, in_=src)
             else:
                 nc.scalar.copy(out=dst, in_=src)
-            return grouped
 
-        def prep_w(lt):
-            ww = w_sb[:, lt, :].bitcast(F32)
-            grouped = turn(ww, 0, "v" if lt % 2 else "s")
-            for g in range(2):
-                c0 = g * G3 + lt * P
-                nc.vector.quantize_mx(
-                    out=wcodes[:, c0:c0 + P].bitcast(FP8X4),
-                    scales=wscl[:, c0:c0 + P],
-                    in_=grouped[:, g * 4 * P:(g + 1) * 4 * P],
-                )
+        groupeds = {}
+        xc = {}
+        pbts = {}
+        pns = {}
+        vs = {}
+        us = {}
+        rzs = {}
 
-        xcodes = {}
+        def a_begin(c):
+            grouped = grp.tile([P, 8 * n], BF16, align_bytes=64)
+            groupeds[c] = grouped
 
-        def prep_x(c):
-            xw = x_sb[c][:].bitcast(F32)
-            for j in range(GRP):
-                grouped = turn(xw, j * (IN // 2), "s")
-                codes = cod.tile([P, 2 * P], U32, align_bytes=64)
-                scl = cod.tile([P, 2 * P], U8, align_bytes=64)
-                nc.vector.quantize_mx(out=codes[:].bitcast(FP8X4), scales=scl[:], in_=grouped[:])
-                xcodes[(c, j)] = (codes, scl)
+        def a_tile(c, j, on_vector):
+            gw = groupeds[c][:].bitcast(F32).rearrange("p (g r u) -> p g r u", g=2, u=2)
+            turn(x_sb[c][:].bitcast(F32), j * (IN // 2), gw[:, :, j * P:(j + 1) * P, :], on_vector)
 
-        rz_t = {}
-        u_t = {}
-        pn_t = {}
+        def a_end(c):
+            codes = cod.tile([P, 2 * n], U32, align_bytes=64)
+            scl = cod.tile([P, 2 * n], U8, align_bytes=64)
+            nc.vector.quantize_mx(out=codes[:].bitcast(FP8X4), scales=scl[:], in_=groupeds[c][:])
+            xc[c] = (codes, scl)
 
-        def e1(c):
-            rz = rzp.tile([P, GRP, 2 * L], F32)
-            nc.vector.tensor_tensor(
-                out=rz[:],
-                in0=g_sb[c][:, :, 0:2 * L],
-                in1=bp_rz[:].unsqueeze(1).to_broadcast([P, GRP, 2 * L]),
-                op=ALU.add,
-            )
-            rz_t[c] = rz
+        def prep_w():
+            for half in range(3):
+                wg = grp.tile([P, 8 * n], BF16, align_bytes=64, tag="grouped")
+                for k in range(2):
+                    lt = 2 * half + k
+                    dst = wg[:, k * 8 * P:(k + 1) * 8 * P].bitcast(F32).rearrange("p (g r u) -> p g r u", g=2, u=2)
+                    turn(w_sb[:, lt, :].bitcast(F32), 0, dst, k == 1)
+                for k in range(2):
+                    lt = 2 * half + k
+                    for g in range(2):
+                        c0 = g * G3 + lt * P
+                        nc.vector.quantize_mx(
+                            out=wcodes[:, c0:c0 + P].bitcast(FP8X4),
+                            scales=wscl[:, c0:c0 + P],
+                            in_=wg[:, (2 * k + g) * 4 * P:(2 * k + g + 1) * 4 * P],
+                        )
 
-        def main(c):
-            rz = rz_t[c]
-            for j in range(GRP):
-                codes, scl = xcodes[(c, j)]
-                prz = pzz.tile([P, 2 * L], F32)
-                if j % 2 == 0:
-                    pn = pnn.tile([P, 2, L], F32)
-                    pn_t[(c, j // 2)] = pn
-                pn = pn_t[(c, j // 2)]
+        def b_rz(c, share_with_vector):
+            codes, scl = xc[c]
+            pbt = pbp.tile([P, 4, n], F32)
+            pbts[c] = pbt
+            for lt in range(4):
+                pt = ppt.tile([P, n], F32)
                 for g in range(2):
-                    lhs = codes[:, g * P:(g + 1) * P].bitcast(FP8X4)
-                    lsc = scl[:, g * P:(g + 1) * P]
+                    c0 = g * G3 + lt * P
                     nc.tensor.matmul_mx(
-                        out=prz[:], lhsT=lhs, lhsT_scale=lsc,
-                        rhs=wcodes[:, g * G3:g * G3 + 2 * L].bitcast(FP8X4),
-                        rhs_scale=wscl[:, g * G3:g * G3 + 2 * L],
+                        out=pt[:],
+                        lhsT=wcodes[:, c0:c0 + P].bitcast(FP8X4), lhsT_scale=wscl[:, c0:c0 + P],
+                        rhs=codes[:, g * n:(g + 1) * n].bitcast(FP8X4), rhs_scale=scl[:, g * n:(g + 1) * n],
                         start=(g == 0), stop=(g == 1),
                     )
-                    nc.tensor.matmul_mx(
-                        out=pn[:, j % 2, :], lhsT=lhs, lhsT_scale=lsc,
-                        rhs=wcodes[:, g * G3 + 2 * L:(g + 1) * G3].bitcast(FP8X4),
-                        rhs_scale=wscl[:, g * G3 + 2 * L:(g + 1) * G3],
-                        start=(g == 0), stop=(g == 1),
-                    )
-                nc.vector.tensor_tensor(out=rz[:, j, :], in0=prz[:], in1=rz[:, j, :], op=ALU.add)
-                nc.scalar.activation(out=rz[:, j, :], in_=rz[:, j, :], func=ACT.Sigmoid)
+                if share_with_vector and lt % 2 == 1:
+                    nc.vector.tensor_scalar_add(out=pbt[:, lt, :], in0=pt[:], scalar1=bias_col[:, lt:lt + 1])
+                else:
+                    nc.scalar.activation(out=pbt[:, lt, :], in_=pt[:], func=ACT.Identity,
+                                         bias=bias_col[:, lt:lt + 1], scale=1.0)
 
-        def mid(c):
-            rz = rz_t[c]
-            u = upl.tile([P, GRP, L], F32)
-            u_t[c] = u
+        def b_n_tensor(c):
+            codes, scl = xc[c]
             for h in range(GRP // 2):
-                js = slice(2 * h, 2 * h + 2)
-                nc.vector.tensor_tensor(out=u[:, js, :], in0=rz[:, js, 0:L], in1=g_sb[c][:, js, 2 * L:G3], op=ALU.mult)
-                nc.vector.tensor_tensor(out=u[:, js, :], in0=pn_t[(c, h)][:], in1=u[:, js, :], op=ALU.add)
+                pn = pnn.tile([P, 2, L], F32)
+                pns[(c, h)] = pn
+                for jj in range(2):
+                    for g in range(2):
+                        c0 = g * n + (2 * h + jj) * P
+                        nc.tensor.matmul_mx(
+                            out=pn[:, jj, :],
+                            lhsT=codes[:, c0:c0 + P].bitcast(FP8X4), lhsT_scale=scl[:, c0:c0 + P],
+                            rhs=wcodes[:, g * G3 + 2 * L:(g + 1) * G3].bitcast(FP8X4),
+                            rhs_scale=wscl[:, g * G3 + 2 * L:(g + 1) * G3],
+                            start=(g == 0), stop=(g == 1),
+                        )
+
+        def b_n_vector(c):
+            v = vpl.tile([P, GRP, L], F32)
+            vs[c] = v
+            for h in range(GRP // 2):
                 nc.vector.tensor_tensor(
-                    out=u[:, js, :],
-                    in0=bp_n[:].unsqueeze(1).to_broadcast([P, 2, L]),
-                    in1=u[:, js, :],
-                    op=ALU.add,
+                    out=v[:, 2 * h:2 * h + 2, :], in0=pns[(c, h)][:],
+                    in1=bn_sb[:].unsqueeze(1).to_broadcast([P, 2, L]), op=ALU.add,
                 )
-                nc.scalar.activation(out=u[:, js, :], in_=u[:, js, :], func=ACT.Tanh)
 
-        def tail(c):
-            rz = rz_t[c]
-            u = u_t[c]
+        def c_begin(c):
+            rz = rzp.tile([P, GRP, 2 * L], F32)
+            rzs[c] = rz
+            u = upl.tile([P, GRP, L], F32)
+            us[c] = u
+
+        def c_tile(c, j):
+            acc = pac.tile([P, 2 * L], F32)
+            nc.tensor.matmul(out=acc[:], lhsT=identb[:], rhs=g_sb[c][:, j, 0:2 * L], start=True, stop=False)
+            for lt in range(4):
+                nc.tensor.matmul(
+                    out=acc[:, lt * P:(lt + 1) * P], lhsT=pbts[c][:, lt, j * P:(j + 1) * P], rhs=ident[:],
+                    is_transpose=True, start=False, stop=(lt == 3),
+                )
+            nc.scalar.activation(out=rzs[c][:, j, :], in_=acc[:], func=ACT.Sigmoid)
+
+        def d_vector(c, h):
+            js = slice(2 * h, 2 * h + 2)
+            nc.vector.tensor_tensor(out=us[c][:, js, :], in0=rzs[c][:, js, 0:L], in1=g_sb[c][:, js, 2 * L:G3], op=ALU.mult)
+            nc.vector.tensor_tensor(out=vs[c][:, js, :], in0=vs[c][:, js, :], in1=us[c][:, js, :], op=ALU.add)
+
+        def d_scalar(c, h):
+            js = slice(2 * h, 2 * h + 2)
+            nc.scalar.activation(out=vs[c][:, js, :], in_=vs[c][:, js, :], func=ACT.Tanh)
+
+        def blend(c, step):
             o = opl.tile([P, GRP, L], F32)
-            if c in V_TAIL_GROUPS:
-                for h in range(GRP // 2):
-                    js = slice(2 * h, 2 * h + 2)
-                    nc.vector.tensor_tensor(out=o[:, js, :], in0=h_sb[c][:, js, :], in1=u[:, js, :], op=ALU.subtract)
-                    nc.vector.tensor_tensor(out=o[:, js, :], in0=o[:, js, :], in1=rz[:, js, L:2 * L], op=ALU.mult)
-                    nc.vector.tensor_tensor(out=o[:, js, :], in0=o[:, js, :], in1=u[:, js, :], op=ALU.add)
-                    nc.sync.dma_start(out=o_v[:, c * GRP + 2 * h:c * GRP + 2 * h + 2, :], in_=o[:, js, :])
-            else:
-                nc.gpsimd.tensor_tensor(out=o[:], in0=h_sb[c][:], in1=u[:], op=ALU.subtract)
-                nc.gpsimd.tensor_tensor(out=o[:], in0=o[:], in1=rz[:, :, L:2 * L], op=ALU.mult)
-                nc.gpsimd.tensor_tensor(out=o[:], in0=o[:], in1=u[:], op=ALU.add)
-                nc.sync.dma_start(out=o_v[:, c * GRP:(c + 1) * GRP, :], in_=o[:])
+            for j0 in range(0, GRP, step):
+                js = slice(j0, j0 + step)
+                nc.vector.tensor_tensor(out=o[:, js, :], in0=h_sb[c][:, js, :], in1=vs[c][:, js, :], op=ALU.subtract)
+                nc.vector.tensor_tensor(out=o[:, js, :], in0=o[:, js, :], in1=rzs[c][:, js, L:2 * L], op=ALU.mult)
+                nc.vector.tensor_tensor(out=o[:, js, :], in0=o[:, js, :], in1=vs[c][:, js, :], op=ALU.add)
+                nc.sync.dma_start(out=o_v[:, c * GRP + j0:c * GRP + j0 + step, :], in_=o[:, js, :])
 
-        e1(0)
-        prep_x(0)
-        for lt in range(WT):
-            prep_w(lt)
-        e1(1)
-        prep_x(1)
-        for c in range(NG):
-            main(c)
-            if c + 2 < NG:
-                e1(c + 2)
-                prep_x(c + 2)
-            mid(c)
-            tail(c)
+        a_begin(0)
+        for j in range(GRP):
+            a_tile(0, j, j % 2 == 1)
+        a_end(0)
+        prep_w()
+        b_rz(0, True)
+        b_n_tensor(0)
+        a_begin(1)
+        for j in range(GRP):
+            a_tile(1, j, j % 2 == 1)
+        a_end(1)
+        load_x(4)
+        load_gh(2)
+
+        for i in range(NG + 1):
+            if i < NG:
+                b_n_vector(i)
+            if i >= 1:
+                blend(i - 1, 2 if i == NG else GRP)
+            if i < NG:
+                c_begin(i)
+                if i + 2 < NG:
+                    a_begin(i + 2)
+                for j in range(GRP):
+                    c_tile(i, j)
+                    if i + 2 < NG:
+                        a_tile(i + 2, j, j == GRP - 1 and i < V_COPY_UNTIL)
+                    if j % 2 == 1:
+                        d_vector(i, j // 2)
+                if i + 2 < NG:
+                    a_end(i + 2)
+                if i + 5 < NG:
+                    load_x(i + 5)
+                if i + 3 < NG:
+                    load_gh(i + 3)
+            if i + 1 < NG:
+                b_rz(i + 1, False)
+                b_n_tensor(i + 1)
+            if i < NG:
+                for h in range(GRP // 2):
+                    d_scalar(i, h)

@@ -49,10 +49,7 @@ def tile_grucellstack_pa_t_kernel(tc, x, h0, gh0, w_ih0, b_ih0, out):
         vpl = ctx.enter_context(tc.tile_pool(name="vpl", bufs=4))
         upl = ctx.enter_context(tc.tile_pool(name="upl", bufs=2))
         opl = ctx.enter_context(tc.tile_pool(name="opl", bufs=3))
-        pxt = ctx.enter_context(tc.psum_pool(name="pxt", bufs=2))
-        ppt = ctx.enter_context(tc.psum_pool(name="ppt", bufs=2))
-        pac = ctx.enter_context(tc.psum_pool(name="pac", bufs=2))
-        pnn = ctx.enter_context(tc.psum_pool(name="pnn", bufs=2))
+        psum = ctx.enter_context(tc.psum_pool(name="psum", bufs=8))
 
         brow = const.tile([P, P], BF16)
         nc.vector.memset(brow[:], 0.0)
@@ -94,11 +91,11 @@ def tile_grucellstack_pa_t_kernel(tc, x, h0, gh0, w_ih0, b_ih0, out):
         load_gh(1)
         load_x(3)
 
-        bt_ps = pxt.tile([P, P], BF16, tag="xt")
+        bt_ps = psum.tile([P, P], BF16, tag="bank")
         nc.tensor.transpose(bt_ps[:], brow[:], identb[:])
         bias_col = const.tile([P, 8], F32)
         nc.vector.tensor_copy(out=bias_col[:, 0:WT], in_=bt_ps[:, 0:WT])
-        bn_ps = pxt.tile([P, L], F32, tag="xt")
+        bn_ps = psum.tile([P, L], F32, tag="bank")
         nc.tensor.matmul(out=bn_ps[:], lhsT=ones[:], rhs=bz[:], start=True, stop=True)
         bn_sb = const.tile([P, L], F32)
         nc.vector.tensor_copy(out=bn_sb[:], in_=bn_ps[:])
@@ -107,7 +104,7 @@ def tile_grucellstack_pa_t_kernel(tc, x, h0, gh0, w_ih0, b_ih0, out):
         wscl = const.tile([P, 2 * G3], U8, align_bytes=64)
 
         def turn(words, col0, dst, on_vector):
-            xt = pxt.tile([P, 4, P], F32)
+            xt = psum.tile([P, 4, P], F32, tag="bank")
             for q in range(4):
                 nc.tensor.transpose(xt[:, q, :], words[:, col0 + q * P:col0 + (q + 1) * P], ident[:])
             src = xt[:].rearrange("p (g u) r -> p g r u", u=2)
@@ -160,7 +157,7 @@ def tile_grucellstack_pa_t_kernel(tc, x, h0, gh0, w_ih0, b_ih0, out):
             pbt = pbp.tile([P, 4, n], F32)
             pbts[c] = pbt
             for lt in range(4):
-                pt = ppt.tile([P, n], F32)
+                pt = psum.tile([P, n], F32, tag="bank")
                 for g in range(2):
                     c0 = g * G3 + lt * P
                     nc.tensor.matmul_mx(
@@ -178,7 +175,7 @@ def tile_grucellstack_pa_t_kernel(tc, x, h0, gh0, w_ih0, b_ih0, out):
         def b_n_tensor(c):
             codes, scl = xc[c]
             for h in range(GRP // 2):
-                pn = pnn.tile([P, 2, L], F32)
+                pn = psum.tile([P, 2, L], F32, tag="bank")
                 pns[(c, h)] = pn
                 for jj in range(2):
                     for g in range(2):
@@ -207,7 +204,7 @@ def tile_grucellstack_pa_t_kernel(tc, x, h0, gh0, w_ih0, b_ih0, out):
             us[c] = u
 
         def c_tile(c, j):
-            acc = pac.tile([P, 2 * L], F32)
+            acc = psum.tile([P, 2 * L], F32, tag="bank")
             nc.tensor.matmul(out=acc[:], lhsT=identb[:], rhs=g_sb[c][:, j, 0:2 * L], start=True, stop=False)
             for lt in range(4):
                 nc.tensor.matmul(

@@ -21,7 +21,6 @@ GRP = 4
 NG = NT // GRP
 WT = G3 // P
 PIN = True
-V_COPY_UNTIL = 4
 
 FLOPS = 2 * B * IN * G3
 
@@ -67,9 +66,11 @@ def tile_grucellstack_pa_t_kernel(tc, x, h0, gh0, w_ih0, b_ih0, out):
         h_sb = {}
         w_sb = const.tile([P, WT, IN], BF16)
 
-        def load_x(c):
+        def load_x(c, pieces):
             xt_in = xin.tile([P, GRP * IN], BF16)
-            nc.sync.dma_start(out=xt_in[:], in_=x_v[:, c * GRP * IN:(c + 1) * GRP * IN])
+            w = GRP * IN // pieces
+            for k in range(pieces):
+                nc.sync.dma_start(out=xt_in[:, k * w:(k + 1) * w], in_=x_v[:, c * GRP * IN + k * w:c * GRP * IN + (k + 1) * w])
             x_sb[c] = xt_in
 
         def load_gh(c):
@@ -82,14 +83,14 @@ def tile_grucellstack_pa_t_kernel(tc, x, h0, gh0, w_ih0, b_ih0, out):
 
         nc.sync.dma_start(out=brow[0:WT, :], in_=b_ih0.rearrange("(r c) -> r c", c=P))
         nc.sync.dma_start(out=bz[0:1, :], in_=b_ih0.rearrange("(o c) -> o c", o=1)[:, 2 * L:G3])
-        load_x(0)
+        load_x(0, 4)
         for i in range(3):
             nc.sync.dma_start(out=w_sb[:, 2 * i:2 * i + 2, :], in_=w_v[:, 2 * i:2 * i + 2, :])
-        load_x(1)
+        load_x(1, 1)
         load_gh(0)
-        load_x(2)
+        load_x(2, 1)
         load_gh(1)
-        load_x(3)
+        load_x(3, 1)
 
         bt_ps = psum.tile([P, P], BF16, tag="bank")
         nc.tensor.transpose(bt_ps[:], brow[:], identb[:])
@@ -120,6 +121,7 @@ def tile_grucellstack_pa_t_kernel(tc, x, h0, gh0, w_ih0, b_ih0, out):
         vs = {}
         us = {}
         rzs = {}
+        outs = {}
 
         def a_begin(c):
             grouped = grp.tile([P, 8 * n], BF16, align_bytes=64)
@@ -188,14 +190,14 @@ def tile_grucellstack_pa_t_kernel(tc, x, h0, gh0, w_ih0, b_ih0, out):
                             start=(g == 0), stop=(g == 1),
                         )
 
-        def b_n_vector(c):
-            v = vpl.tile([P, GRP, L], F32)
-            vs[c] = v
-            for h in range(GRP // 2):
-                nc.vector.tensor_tensor(
-                    out=v[:, 2 * h:2 * h + 2, :], in0=pns[(c, h)][:],
-                    in1=bn_sb[:].unsqueeze(1).to_broadcast([P, 2, L]), op=ALU.add,
-                )
+        def b_n_vector(c, h):
+            if h == 0:
+                v = vpl.tile([P, GRP, L], F32)
+                vs[c] = v
+            nc.vector.tensor_tensor(
+                out=vs[c][:, 2 * h:2 * h + 2, :], in0=pns[(c, h)][:],
+                in1=bn_sb[:].unsqueeze(1).to_broadcast([P, 2, L]), op=ALU.add,
+            )
 
         def c_begin(c):
             rz = rzp.tile([P, GRP, 2 * L], F32)
@@ -213,23 +215,31 @@ def tile_grucellstack_pa_t_kernel(tc, x, h0, gh0, w_ih0, b_ih0, out):
                 )
             nc.scalar.activation(out=rzs[c][:, j, :], in_=acc[:], func=ACT.Sigmoid)
 
-        def d_vector(c, h):
+        def e4(c, h):
             js = slice(2 * h, 2 * h + 2)
             nc.vector.tensor_tensor(out=us[c][:, js, :], in0=rzs[c][:, js, 0:L], in1=g_sb[c][:, js, 2 * L:G3], op=ALU.mult)
+
+        def e6(c, h):
+            js = slice(2 * h, 2 * h + 2)
             nc.vector.tensor_tensor(out=vs[c][:, js, :], in0=vs[c][:, js, :], in1=us[c][:, js, :], op=ALU.add)
 
         def d_scalar(c, h):
             js = slice(2 * h, 2 * h + 2)
             nc.scalar.activation(out=vs[c][:, js, :], in_=vs[c][:, js, :], func=ACT.Tanh)
 
-        def blend(c, step):
-            o = opl.tile([P, GRP, L], F32)
-            for j0 in range(0, GRP, step):
-                js = slice(j0, j0 + step)
+        def blend_op(c, h, k):
+            if h == 0 and k == 0:
+                o_new = opl.tile([P, GRP, L], F32)
+                outs[c] = o_new
+            js = slice(2 * h, 2 * h + 2)
+            o = outs[c]
+            if k == 0:
                 nc.vector.tensor_tensor(out=o[:, js, :], in0=h_sb[c][:, js, :], in1=vs[c][:, js, :], op=ALU.subtract)
+            elif k == 1:
                 nc.vector.tensor_tensor(out=o[:, js, :], in0=o[:, js, :], in1=rzs[c][:, js, L:2 * L], op=ALU.mult)
+            else:
                 nc.vector.tensor_tensor(out=o[:, js, :], in0=o[:, js, :], in1=vs[c][:, js, :], op=ALU.add)
-                nc.sync.dma_start(out=o_v[:, c * GRP + j0:c * GRP + j0 + step, :], in_=o[:, js, :])
+                nc.sync.dma_start(out=o_v[:, c * GRP + 2 * h:c * GRP + 2 * h + 2, :], in_=o[:, js, :])
 
         a_begin(0)
         for j in range(GRP):
@@ -238,18 +248,24 @@ def tile_grucellstack_pa_t_kernel(tc, x, h0, gh0, w_ih0, b_ih0, out):
         prep_w()
         b_rz(0, True)
         b_n_tensor(0)
+        b_n_vector(0, 0)
+        b_n_vector(0, 1)
         a_begin(1)
         for j in range(GRP):
             a_tile(1, j, j % 2 == 1)
         a_end(1)
-        load_x(4)
+        load_x(4, 1)
         load_gh(2)
 
         for i in range(NG + 1):
-            if i < NG:
-                b_n_vector(i)
+            if 1 <= i < NG:
+                b_n_vector(i, 0)
+                b_n_vector(i, 1)
             if i >= 1:
-                blend(i - 1, 2 if i == NG else GRP)
+                for k in range(2):
+                    blend_op(i - 1, 0, k)
+                    blend_op(i - 1, 1, k)
+                blend_op(i - 1, 0, 2)
             if i < NG:
                 c_begin(i)
                 if i + 2 < NG:
@@ -257,15 +273,23 @@ def tile_grucellstack_pa_t_kernel(tc, x, h0, gh0, w_ih0, b_ih0, out):
                 for j in range(GRP):
                     c_tile(i, j)
                     if i + 2 < NG:
-                        a_tile(i + 2, j, j == GRP - 1 and i < V_COPY_UNTIL)
-                    if j % 2 == 1:
-                        d_vector(i, j // 2)
-                if i + 2 < NG:
-                    a_end(i + 2)
+                        a_tile(i + 2, j, False)
+                    if j == 1:
+                        e4(i, 0)
+                        if i >= 1:
+                            blend_op(i - 1, 1, 2)
+                        e6(i, 0)
+                    if j == 3:
+                        e4(i, 1)
+                        if i + 2 < NG:
+                            a_end(i + 2)
+                        e6(i, 1)
                 if i + 5 < NG:
-                    load_x(i + 5)
+                    load_x(i + 5, 1)
                 if i + 3 < NG:
                     load_gh(i + 3)
+            else:
+                blend_op(i - 1, 1, 2)
             if i + 1 < NG:
                 b_rz(i + 1, False)
                 b_n_tensor(i + 1)

from contextlib import ExitStack

import concourse.mybir as mybir
from concourse.masks import make_identity

F32 = mybir.dt.float32
BF16 = mybir.dt.bfloat16
U32 = mybir.dt.uint32
U8 = mybir.dt.uint8
FP8X4 = mybir.dt.float8_e4m3fn_x4
ACT = mybir.ActivationFunctionType
ALU = mybir.AluOpType

P = 128
B = 4096
IN = 1024
L = 256
G3 = 3 * L
NT = B // P
GRP = 4
NG = NT // GRP
WT = G3 // P
PIN = True

FLOPS = 2 * B * IN * G3


def tile_grucellstack_pa_t_kernel(tc, x, h0, gh0, w_ih0, b_ih0, out):
    nc = tc.nc
    x_v = x.rearrange("(p t) k -> p (t k)", t=NT)
    g_v = gh0.rearrange("(p t) c -> p t c", t=NT)
    h_v = h0.rearrange("(p t) c -> p t c", t=NT)
    o_v = out.rearrange("(p t) c -> p t c", t=NT)
    w_v = w_ih0.rearrange("(t p) k -> p t k", p=P)
    n = GRP * P

    with ExitStack() as ctx:
        if PIN:
            ctx.enter_context(tc.manual_schedule())
        const = ctx.enter_context(tc.tile_pool(name="const", bufs=1))
        xin = ctx.enter_context(tc.tile_pool(name="xin", bufs=4))
        gin = ctx.enter_context(tc.tile_pool(name="gin", bufs=NG))
        hin = ctx.enter_context(tc.tile_pool(name="hin", bufs=NG))
        grp = ctx.enter_context(tc.tile_pool(name="grp", bufs=2))
        cod = ctx.enter_context(tc.tile_pool(name="cod", bufs=3))
        pbp = ctx.enter_context(tc.tile_pool(name="pbp", bufs=2))
        rzp = ctx.enter_context(tc.tile_pool(name="rzp", bufs=3))
        vpl = ctx.enter_context(tc.tile_pool(name="vpl", bufs=4))
        upl = ctx.enter_context(tc.tile_pool(name="upl", bufs=2))
        opl = ctx.enter_context(tc.tile_pool(name="opl", bufs=3))
        psum = ctx.enter_context(tc.psum_pool(name="psum", bufs=8))

        brow = const.tile([P, P], BF16)
        nc.vector.memset(brow[:], 0.0)
        bz = const.tile([P, L], BF16)
        nc.vector.memset(bz[:], 0.0)
        ones = const.tile([P, P], BF16)
        nc.vector.memset(ones[:], 1.0)
        ident = const.tile([P, P], F32)
        make_identity(nc, ident[:])
        identb = const.tile([P, P], BF16)
        make_identity(nc, identb[:])

        x_sb = {}
        g_sb = {}
        h_sb = {}
        w_sb = const.tile([P, WT, IN], BF16)

        def load_x(c, pieces):
            xt_in = xin.tile([P, GRP * IN], BF16)
            w = GRP * IN // pieces
            for k in range(pieces):
                nc.sync.dma_start(out=xt_in[:, k * w:(k + 1) * w], in_=x_v[:, c * GRP * IN + k * w:c * GRP * IN + (k + 1) * w])
            x_sb[c] = xt_in

        def load_gh(c):
            gt_in = gin.tile([P, GRP, G3], BF16)
            nc.sync.dma_start(out=gt_in[:], in_=g_v[:, c * GRP:(c + 1) * GRP, :])
            g_sb[c] = gt_in
            ht_in = hin.tile([P, GRP, L], BF16)
            nc.sync.dma_start(out=ht_in[:], in_=h_v[:, c * GRP:(c + 1) * GRP, :])
            h_sb[c] = ht_in

        nc.sync.dma_start(out=brow[0:WT, :], in_=b_ih0.rearrange("(r c) -> r c", c=P))
        nc.sync.dma_start(out=bz[0:1, :], in_=b_ih0.rearrange("(o c) -> o c", o=1)[:, 2 * L:G3])
        load_x(0, 4)
        for i in range(3):
            nc.sync.dma_start(out=w_sb[:, 2 * i:2 * i + 2, :], in_=w_v[:, 2 * i:2 * i + 2, :])
        load_x(1, 1)
        load_gh(0)
        load_x(2, 1)
        load_gh(1)
        load_x(3, 1)

        bt_ps = psum.tile([P, P], BF16, tag="bank")
        nc.tensor.transpose(bt_ps[:], brow[:], identb[:])
        bias_col = const.tile([P, 8], F32)
        nc.vector.tensor_copy(out=bias_col[:, 0:WT], in_=bt_ps[:, 0:WT])
        bn_ps = psum.tile([P, L], F32, tag="bank")
        nc.tensor.matmul(out=bn_ps[:], lhsT=ones[:], rhs=bz[:], start=True, stop=True)
        bn_sb = const.tile([P, L], F32)
        nc.vector.tensor_copy(out=bn_sb[:], in_=bn_ps[:])

        wcodes = const.tile([P, 2 * G3], U32, align_bytes=64)
        wscl = const.tile([P, 2 * G3], U8, align_bytes=64)

        def turn(words, col0, dst, on_vector):
            xt = psum.tile([P, 4, P], F32, tag="bank")
            for q in range(4):
                nc.tensor.transpose(xt[:, q, :], words[:, col0 + q * P:col0 + (q + 1) * P], ident[:])
            src = xt[:].rearrange("p (g u) r -> p g r u", u=2)
            if on_vector:
                nc.vector.tensor_copy(out=dst, in_=src)
            else:
                nc.scalar.copy(out=dst, in_=src)

        groupeds = {}
        xc = {}
        pbts = {}
        pns = {}
        vs = {}
        us = {}
        rzs = {}
        outs = {}

        def a_begin(c):
            grouped = grp.tile([P, 8 * n], BF16, align_bytes=64)
            groupeds[c] = grouped

        def a_tile(c, j, on_vector):
            gw = groupeds[c][:].bitcast(F32).rearrange("p (g r u) -> p g r u", g=2, u=2)
            turn(x_sb[c][:].bitcast(F32), j * (IN // 2), gw[:, :, j * P:(j + 1) * P, :], on_vector)

        def a_end(c):
            codes = cod.tile([P, 2 * n], U32, align_bytes=64)
            scl = cod.tile([P, 2 * n], U8, align_bytes=64)
            nc.vector.quantize_mx(out=codes[:].bitcast(FP8X4), scales=scl[:], in_=groupeds[c][:])
            xc[c] = (codes, scl)

        def prep_w():
            for half in range(3):
                wg = grp.tile([P, 8 * n], BF16, align_bytes=64, tag="grouped")
                for k in range(2):
                    lt = 2 * half + k
                    dst = wg[:, k * 8 * P:(k + 1) * 8 * P].bitcast(F32).rearrange("p (g r u) -> p g r u", g=2, u=2)
                    turn(w_sb[:, lt, :].bitcast(F32), 0, dst, k == 1)
                for k in range(2):
                    lt = 2 * half + k
                    for g in range(2):
                        c0 = g * G3 + lt * P
                        nc.vector.quantize_mx(
                            out=wcodes[:, c0:c0 + P].bitcast(FP8X4),
                            scales=wscl[:, c0:c0 + P],
                            in_=wg[:, (2 * k + g) * 4 * P:(2 * k + g + 1) * 4 * P],
                        )

        def b_rz(c, share_with_vector):
            codes, scl = xc[c]
            pbt = pbp.tile([P, 4, n], F32)
            pbts[c] = pbt
            for lt in range(4):
                pt = psum.tile([P, n], F32, tag="bank")
                for g in range(2):
                    c0 = g * G3 + lt * P
                    nc.tensor.matmul_mx(
                        out=pt[:],
                        lhsT=wcodes[:, c0:c0 + P].bitcast(FP8X4), lhsT_scale=wscl[:, c0:c0 + P],
                        rhs=codes[:, g * n:(g + 1) * n].bitcast(FP8X4), rhs_scale=scl[:, g * n:(g + 1) * n],
                        start=(g == 0), stop=(g == 1),
                    )
                if share_with_vector and lt % 2 == 1:
                    nc.vector.tensor_scalar_add(out=pbt[:, lt, :], in0=pt[:], scalar1=bias_col[:, lt:lt + 1])
                else:
                    nc.scalar.activation(out=pbt[:, lt, :], in_=pt[:], func=ACT.Identity,
                                         bias=bias_col[:, lt:lt + 1], scale=1.0)

        def b_n_tensor(c):
            codes, scl = xc[c]
            for h in range(GRP // 2):
                pn = psum.tile([P, 2, L], F32, tag="bank")
                pns[(c, h)] = pn
                for jj in range(2):
                    for g in range(2):
                        c0 = g * n + (2 * h + jj) * P
                        nc.tensor.matmul_mx(
                            out=pn[:, jj, :],
                            lhsT=codes[:, c0:c0 + P].bitcast(FP8X4), lhsT_scale=scl[:, c0:c0 + P],
                            rhs=wcodes[:, g * G3 + 2 * L:(g + 1) * G3].bitcast(FP8X4),
                            rhs_scale=wscl[:, g * G3 + 2 * L:(g + 1) * G3],
                            start=(g == 0), stop=(g == 1),
                        )

        def b_n_vector(c, h):
            if h == 0:
                v = vpl.tile([P, GRP, L], F32)
                vs[c] = v
            nc.vector.tensor_tensor(
                out=vs[c][:, 2 * h:2 * h + 2, :], in0=pns[(c, h)][:],
                in1=bn_sb[:].unsqueeze(1).to_broadcast([P, 2, L]), op=ALU.add,
            )

        def c_begin(c):
            rz = rzp.tile([P, GRP, 2 * L], F32)
            rzs[c] = rz
            u = upl.tile([P, GRP, L], F32)
            us[c] = u

        def c_tile(c, j):
            acc = psum.tile([P, 2 * L], F32, tag="bank")
            nc.tensor.matmul(out=acc[:], lhsT=identb[:], rhs=g_sb[c][:, j, 0:2 * L], start=True, stop=False)
            for lt in range(4):
                nc.tensor.matmul(
                    out=acc[:, lt * P:(lt + 1) * P], lhsT=pbts[c][:, lt, j * P:(j + 1) * P], rhs=ident[:],
                    is_transpose=True, start=False, stop=(lt == 3),
                )
            nc.scalar.activation(out=rzs[c][:, j, :], in_=acc[:], func=ACT.Sigmoid)

        def e4(c, h):
            js = slice(2 * h, 2 * h + 2)
            nc.vector.tensor_tensor(out=us[c][:, js, :], in0=rzs[c][:, js, 0:L], in1=g_sb[c][:, js, 2 * L:G3], op=ALU.mult)

        def e6(c, h):
            js = slice(2 * h, 2 * h + 2)
            nc.vector.tensor_tensor(out=vs[c][:, js, :], in0=vs[c][:, js, :], in1=us[c][:, js, :], op=ALU.add)

        def d_scalar(c, h):
            js = slice(2 * h, 2 * h + 2)
            nc.scalar.activation(out=vs[c][:, js, :], in_=vs[c][:, js, :], func=ACT.Tanh)

        def blend_op(c, h, k):
            if h == 0 and k == 0:
                o_new = opl.tile([P, GRP, L], F32)
                outs[c] = o_new
            js = slice(2 * h, 2 * h + 2)
            o = outs[c]
            if k == 0:
                nc.vector.tensor_tensor(out=o[:, js, :], in0=h_sb[c][:, js, :], in1=vs[c][:, js, :], op=ALU.subtract)
            elif k == 1:
                nc.vector.tensor_tensor(out=o[:, js, :], in0=o[:, js, :], in1=rzs[c][:, js, L:2 * L], op=ALU.mult)
            else:
                nc.vector.tensor_tensor(out=o[:, js, :], in0=o[:, js, :], in1=vs[c][:, js, :], op=ALU.add)
                nc.sync.dma_start(out=o_v[:, c * GRP + 2 * h:c * GRP + 2 * h + 2, :], in_=o[:, js, :])

        a_begin(0)
        for j in range(GRP):
            a_tile(0, j, j % 2 == 1)
        a_end(0)
        prep_w()
        b_rz(0, True)
        b_n_tensor(0)
        b_n_vector(0, 0)
        b_n_vector(0, 1)
        a_begin(1)
        for j in range(GRP):
            a_tile(1, j, j % 2 == 1)
        a_end(1)
        load_x(4, 1)
        load_gh(2)

        for i in range(NG + 1):
            if 1 <= i < NG:
                b_n_vector(i, 0)
                b_n_vector(i, 1)
            if i >= 1:
                for k in range(2):
                    blend_op(i - 1, 0, k)
                    blend_op(i - 1, 1, k)
                blend_op(i - 1, 0, 2)
            if i < NG:
                c_begin(i)
                if i + 2 < NG:
                    a_begin(i + 2)
                for j in range(GRP):
                    c_tile(i, j)
                    if i + 2 < NG:
                        a_tile(i + 2, j, False)
                    if j == 1:
                        e4(i, 0)
                        if i >= 1:
                            blend_op(i - 1, 1, 2)
                        e6(i, 0)
                    if j == 3:
                        e4(i, 1)
                        if i + 2 < NG:
                            a_end(i + 2)
                        e6(i, 1)
                if i + 5 < NG:
                    load_x(i + 5, 1)
                if i + 3 < NG:
                    load_gh(i + 3)
            else:
                blend_op(i - 1, 1, 2)
            if i + 1 < NG:
                b_rz(i + 1, False)
                b_n_tensor(i + 1)
            if i < NG:
                for h in range(GRP // 2):
                    d_scalar(i, h)
